import numpy as np
import ml_dtypes


def mxq(x, axis, fmt="e4m3"):
    dtype, down = {"e4m3": (ml_dtypes.float8_e4m3fn, 7), "e5m2": (ml_dtypes.float8_e5m2, 14)}[fmt]
    v = np.moveaxis(np.asarray(x, np.float32).astype(ml_dtypes.bfloat16).astype(np.float64), axis, -1)
    blocks = v.reshape(v.shape[:-1] + (-1, 32))
    amax = np.abs(blocks).max(-1, keepdims=True)
    byte = np.maximum(np.where(amax > 0, np.frexp(amax)[1] - 1 + 127, 0) - down, 1)
    scale = np.exp2(byte - 127.0)
    codes = (blocks / scale).astype(np.float32).astype(dtype).astype(np.float64)
    return np.moveaxis((codes * scale).reshape(v.shape), -1, axis)


WIDE = False


def mx_kscale(k):
    if not WIDE:
        return np.ones(k)
    levels = np.array([10, -10, 5, -5, 0])
    if k % 512:
        return np.exp2(np.random.permutation(np.resize(levels, k // 32))).repeat(32)
    a = np.empty((k // 512, 16))
    for p in range(k // 512):
        a[p, :8] = np.random.permutation(np.resize(levels, 8))
        for g in range(8):
            far = levels[np.abs(levels - a[p, g]) >= 10]
            a[p, g + 8] = far[np.random.randint(len(far))]
    return np.exp2(a.ravel()).repeat(32)


BF16 = ml_dtypes.bfloat16


def bf(x):
    return np.asarray(x, np.float32).astype(BF16)


def f64(x):
    return np.asarray(x).astype(np.float64)


S, B, D, H, F = 512, 2, 1024, 2, 2048
HD = D // H
EPS = 1e-8


def rmsnorm(x, w):
    ms = np.mean(x * x, axis=-1, keepdims=True)
    return w * (x / np.sqrt(ms + EPS))


def heads(t):
    return t.reshape(S, B, H, HD).transpose(1, 2, 0, 3)


def setup_inputs():
    s = mx_kscale(D)
    return {"x": bf(np.random.standard_normal((S, B, D))),
            "w_norm1": bf((1.0 + 0.1 * np.random.standard_normal(D)) * s),
            "in_proj_w": bf(np.random.standard_normal((3 * D, D)) / np.sqrt(D) / s[None, :]),
            "in_proj_b": bf(np.random.standard_normal(3 * D) * 0.3)}


def reference(x, w_norm1, in_proj_w, in_proj_b):
    h = rmsnorm(f64(x), f64(w_norm1))
    qkv = (mxq(h, 2, "e4m3") @ mxq(f64(in_proj_w), 1, "e4m3").T) + f64(in_proj_b)
    q, k, v = np.split(qkv, 3, axis=-1)
    return heads(q), heads(k), heads(v)

@@ -1,0 +1,226 @@
+from contextlib import ExitStack
+
+import concourse.mybir as mybir
+from concourse.masks import make_identity
+
+BF16 = mybir.dt.bfloat16
+F32 = mybir.dt.float32
+U32 = mybir.dt.uint32
+U8 = mybir.dt.uint8
+FP8X4 = mybir.dt.float8_e4m3fn_x4
+ACT = mybir.ActivationFunctionType
+ALU = mybir.AluOpType
+
+P = 128
+SEQ, BATCH, D, HEADS = 512, 2, 1024, 2
+HEAD_DIM = D // HEADS
+EPS = 1e-8
+
+K_PASS = 4 * P
+PASSES = D // K_PASS
+WORDS = D // 2
+SEQ_TILES = SEQ // P
+TOKEN_TILES = BATCH * SEQ_TILES
+CHUNKS = 3 * HEADS
+ROW_TILES = HEAD_DIM // P
+STORE_TILES = 2
+
+FLOPS = 2 * SEQ * BATCH * D * 3 * D
+
+
+def tile_transformerblock_pa_kernel(
+    tc, x, w_norm1, in_proj_w, in_proj_b, out_0, out_1, out_2
+):
+    nc = tc.nc
+    outs = (out_0, out_1, out_2)
+    x_view = x.rearrange("(p i) b d -> p b i d", i=SEQ_TILES)
+
+    with ExitStack() as ctx:
+        const = ctx.enter_context(tc.tile_pool(name="const", bufs=1))
+        keep = ctx.enter_context(tc.tile_pool(name="keep", bufs=1))
+        stage = ctx.enter_context(tc.tile_pool(name="stage", bufs=2))
+        results = ctx.enter_context(tc.tile_pool(name="results", bufs=6))
+        turned = ctx.enter_context(tc.psum_pool(name="turned", bufs=4))
+        sums = ctx.enter_context(tc.psum_pool(name="sums", bufs=4))
+        ctx.enter_context(tc.manual_schedule())
+
+        eps = const.tile([P, 1], F32)
+        nc.vector.memset(eps[:], EPS)
+        table_warm = const.tile([P, 1], F32)
+        nc.scalar.activation(out=table_warm[:], in_=eps[:], func=ACT.Sqrt)
+        gain_row = const.tile([P, D], BF16)
+        nc.vector.memset(gain_row[:], 0.0)
+        ones = const.tile([P, P], BF16)
+        nc.vector.memset(ones[:], 1.0)
+        ident = const.tile([P, P], F32)
+        make_identity(nc, ident[:])
+
+        x_sb = keep.tile([P, TOKEN_TILES, D], BF16)
+        w_sb = keep.tile([P, CHUNKS, ROW_TILES, D], BF16)
+        bias_all = keep.tile([P, 3 * D], BF16)
+
+        def load_weights(c):
+            rows = in_proj_w[c * HEAD_DIM : (c + 1) * HEAD_DIM, :]
+            nc.sync.dma_start(
+                out=w_sb[:, c, :, :], in_=rows.rearrange("(a p) k -> p a k", p=P)
+            )
+
+        nc.sync.dma_start(out=gain_row[0:1, :], in_=w_norm1.unsqueeze(0))
+        for i in range(SEQ_TILES):
+            nc.sync.dma_start(out=x_sb[:, i, :], in_=x_view[:, 0, i, :])
+        load_weights(0)
+        load_weights(1)
+        nc.sync.dma_start(out=bias_all[:], in_=in_proj_b.partition_broadcast(P))
+        nc.sync.dma_start(out=x_sb[:, SEQ_TILES:, :], in_=x_view[:, 1, :, :])
+        for c in range(2, CHUNKS):
+            load_weights(c)
+
+        gain_all = const.tile([P, D], BF16)
+        for half in range(D // HEAD_DIM):
+            cols = slice(half * HEAD_DIM, (half + 1) * HEAD_DIM)
+            spread = turned.tile([P, HEAD_DIM], F32, tag="turned")
+            nc.tensor.matmul(spread[:], lhsT=ones[:], rhs=gain_row[:, cols], start=True, stop=True)
+            nc.vector.tensor_copy(out=gain_all[:, cols], in_=spread[:])
+
+        squares = keep.tile([P, TOKEN_TILES, D], BF16)
+        mean_sq = keep.tile([P, TOKEN_TILES], F32)
+        rms = keep.tile([P, TOKEN_TILES], F32)
+        inv_rms = keep.tile([P, TOKEN_TILES], F32)
+        h_sb = keep.tile([P, TOKEN_TILES, D], BF16)
+        h_codes = keep.tile([P, TOKEN_TILES, PASSES * P], U32, align_bytes=64)
+        h_scales = keep.tile([P, TOKEN_TILES, PASSES * P], U8, align_bytes=64)
+        w_codes = keep.tile([P, CHUNKS, PASSES * HEAD_DIM], U32, align_bytes=64)
+        w_scales = keep.tile([P, CHUNKS, PASSES * HEAD_DIM], U8, align_bytes=64)
+        h_grouped = {}
+        w_grouped = {}
+
+        def normalise(j):
+            nc.scalar.activation(
+                out=squares[:, j, :],
+                in_=x_sb[:, j, :],
+                func=ACT.Square,
+                scale=D**-0.5,
+                accum_out=mean_sq[:, j : j + 1],
+            )
+            nc.scalar.activation(
+                out=rms[:, j : j + 1], in_=mean_sq[:, j : j + 1], func=ACT.Sqrt, bias=eps[:, 0:1]
+            )
+            nc.vector.reciprocal(out=inv_rms[:, j : j + 1], in_=rms[:, j : j + 1])
+            nc.vector.scalar_tensor_tensor(
+                out=h_sb[:, j, :],
+                in0=x_sb[:, j, :],
+                scalar=inv_rms[:, j : j + 1],
+                in1=gain_all[:],
+                op0=ALU.mult,
+                op1=ALU.mult,
+            )
+
+        def turn_tokens(j):
+            words = h_sb[:, j, :].bitcast(F32)
+            bank = turned.tile([P, 2 * PASSES, P], F32, tag="turned")
+            for s in range(2 * PASSES):
+                g, u = divmod(s, 2)
+                nc.tensor.transpose(
+                    bank[:, s, :], words[:, 2 * g * P + u : 2 * (g + 1) * P : 2], ident[:]
+                )
+            grouped = stage.tile([P, PASSES, P, 4], BF16, align_bytes=64, tag="h_grouped")
+            nc.scalar.copy(
+                out=grouped[:].bitcast(F32),
+                in_=bank[:].rearrange("p (g u) r -> p g r u", u=2),
+            )
+            h_grouped[j] = grouped
+
+        def quantise_tokens(j):
+            nc.vector.quantize_mx(
+                out=h_codes[:, j, :].bitcast(FP8X4),
+                scales=h_scales[:, j, :],
+                in_=h_grouped[j][:].rearrange("p g r t -> p (g r t)"),
+            )
+
+        def turn_weights(c):
+            words = w_sb[:, c, :, :].bitcast(F32)
+            grouped = stage.tile([P, PASSES, HEAD_DIM, 4], BF16, align_bytes=64, tag="w_grouped")
+            grouped_words = grouped[:].bitcast(F32)
+            for g in range(PASSES):
+                for pair in range(ROW_TILES // 2):
+                    bank = turned.tile([P, 4, P], F32, tag="turned")
+                    for a in range(2):
+                        for u in range(2):
+                            nc.tensor.transpose(
+                                bank[:, 2 * a + u, :],
+                                words[:, 2 * pair + a, 2 * g * P + u : 2 * (g + 1) * P : 2],
+                                ident[:],
+                            )
+                    nc.scalar.copy(
+                        out=grouped_words[:, g, pair * 2 * P : (pair + 1) * 2 * P, :].rearrange(
+                            "p (a r) u -> p a r u", a=2
+                        ),
+                        in_=bank[:].rearrange("p (a u) r -> p a r u", u=2),
+                    )
+            w_grouped[c] = grouped
+
+        def quantise_weights(c):
+            nc.vector.quantize_mx(
+                out=w_codes[:, c, :].bitcast(FP8X4),
+                scales=w_scales[:, c, :],
+                in_=w_grouped[c][:].rearrange("p g n t -> p (g n t)"),
+            )
+
+        def project(c, b, part):
+            res = results.tile([P, STORE_TILES, HEAD_DIM], F32, tag="res")
+            first = part * STORE_TILES
+            for n in range(STORE_TILES):
+                j = b * SEQ_TILES + first + n
+                acc = sums.tile([P, HEAD_DIM], F32, tag="acc")
+                for g in range(PASSES):
+                    nc.tensor.matmul_mx(
+                        out=acc[:],
+                        lhsT=h_codes[:, j, g * P : (g + 1) * P].bitcast(FP8X4),
+                        lhsT_scale=h_scales[:, j, g * P : (g + 1) * P],
+                        rhs=w_codes[:, c, g * HEAD_DIM : (g + 1) * HEAD_DIM].bitcast(FP8X4),
+                        rhs_scale=w_scales[:, c, g * HEAD_DIM : (g + 1) * HEAD_DIM],
+                        start=(g == 0),
+                        stop=(g == PASSES - 1),
+                    )
+                nc.vector.tensor_tensor(
+                    out=res[:, n, :],
+                    in0=acc[:],
+                    in1=bias_all[:, c * HEAD_DIM : (c + 1) * HEAD_DIM],
+                    op=ALU.add,
+                )
+            head = outs[c // HEADS][b, c % HEADS].rearrange("(p i) d -> p i d", i=SEQ_TILES)
+            nc.sync.dma_start(out=head[:, first : first + STORE_TILES, :], in_=res[:])
+
+        normalise(0)
+        normalise(1)
+        normalise(2)
+        turn_tokens(0)
+        normalise(3)
+        turn_tokens(1)
+        turn_weights(0)
+        quantise_tokens(0)
+        quantise_tokens(1)
+        turn_tokens(2)
+        turn_tokens(3)
+        quantise_weights(0)
+        quantise_tokens(2)
+        quantise_tokens(3)
+
+        for c in range(CHUNKS):
+            late = SEQ_TILES + c - 2
+            if c + 1 < CHUNKS:
+                turn_weights(c + 1)
+            if c >= 2:
+                turn_tokens(late)
+            project(c, 0, 0)
+            if c + 1 < CHUNKS:
+                quantise_weights(c + 1)
+            project(c, 0, 1)
+            if c >= 2:
+                quantise_tokens(late)
+            if c < SEQ_TILES:
+                normalise(SEQ_TILES + c)
+
+        for c in range(CHUNKS):
+            for part in range(SEQ_TILES // STORE_TILES):
+                project(c, 1, part)

@@ -47,9 +47,9 @@ def tile_transformerblock_pa_kernel(
         eps = const.tile([P, 1], F32)
         nc.vector.memset(eps[:], EPS)
         table_warm = const.tile([P, 1], F32)
-        nc.scalar.activation(out=table_warm[:], in_=eps[:], func=ACT.Sqrt)
+        nc.scalar.activation(out=table_warm[:], in_=eps[:], func=ACT.Abs_reciprocal_sqrt)
         gain_row = const.tile([P, D], BF16)
-        nc.vector.memset(gain_row[:], 0.0)
+        nc.vector.memset(gain_row[:].bitcast(F32), 0.0)
         ones = const.tile([P, P], BF16)
         nc.vector.memset(ones[:], 1.0)
         ident = const.tile([P, P], F32)
@@ -65,26 +65,35 @@ def tile_transformerblock_pa_kernel(
                 out=w_sb[:, c, :, :], in_=rows.rearrange("(a p) k -> p a k", p=P)
             )
 
+        nc.sync.dma_start(out=x_sb[:, 0, :], in_=x_view[:, 0, 0, :])
         nc.sync.dma_start(out=gain_row[0:1, :], in_=w_norm1.unsqueeze(0))
-        for i in range(SEQ_TILES):
+        for i in range(1, SEQ_TILES):
             nc.sync.dma_start(out=x_sb[:, i, :], in_=x_view[:, 0, i, :])
         load_weights(0)
         load_weights(1)
         nc.sync.dma_start(out=bias_all[:], in_=in_proj_b.partition_broadcast(P))
-        nc.sync.dma_start(out=x_sb[:, SEQ_TILES:, :], in_=x_view[:, 1, :, :])
-        for c in range(2, CHUNKS):
-            load_weights(c)
+        load_weights(2)
+        nc.sync.dma_start(
+            out=x_sb[:, SEQ_TILES + 0 : SEQ_TILES + 2, :], in_=x_view[:, 1, 0 : 2, :]
+        )
+        load_weights(3)
+        nc.sync.dma_start(
+            out=x_sb[:, SEQ_TILES + 2 : SEQ_TILES + 4, :], in_=x_view[:, 1, 2 : 4, :]
+        )
+        load_weights(4)
+        load_weights(5)
 
         gain_all = const.tile([P, D], BF16)
+        spread = turned.tile([P, D], BF16, tag="turned")
         for half in range(D // HEAD_DIM):
             cols = slice(half * HEAD_DIM, (half + 1) * HEAD_DIM)
-            spread = turned.tile([P, HEAD_DIM], F32, tag="turned")
-            nc.tensor.matmul(spread[:], lhsT=ones[:], rhs=gain_row[:, cols], start=True, stop=True)
-            nc.vector.tensor_copy(out=gain_all[:, cols], in_=spread[:])
+            nc.tensor.matmul(
+                spread[:, cols], lhsT=ones[:], rhs=gain_row[:, cols], start=True, stop=True
+            )
+        nc.vector.tensor_copy(out=gain_all[:], in_=spread[:])
 
         squares = keep.tile([P, TOKEN_TILES, D], BF16)
         mean_sq = keep.tile([P, TOKEN_TILES], F32)
-        rms = keep.tile([P, TOKEN_TILES], F32)
         inv_rms = keep.tile([P, TOKEN_TILES], F32)
         h_sb = keep.tile([P, TOKEN_TILES, D], BF16)
         h_codes = keep.tile([P, TOKEN_TILES, PASSES * P], U32, align_bytes=64)
@@ -103,9 +112,11 @@ def tile_transformerblock_pa_kernel(
                 accum_out=mean_sq[:, j : j + 1],
             )
             nc.scalar.activation(
-                out=rms[:, j : j + 1], in_=mean_sq[:, j : j + 1], func=ACT.Sqrt, bias=eps[:, 0:1]
+                out=inv_rms[:, j : j + 1],
+                in_=mean_sq[:, j : j + 1],
+                func=ACT.Abs_reciprocal_sqrt,
+                bias=eps[:, 0:1],
             )
-            nc.vector.reciprocal(out=inv_rms[:, j : j + 1], in_=rms[:, j : j + 1])
             nc.vector.scalar_tensor_tensor(
                 out=h_sb[:, j, :],
                 in0=x_sb[:, j, :],
@@ -182,12 +193,8 @@ def tile_transformerblock_pa_kernel(
                         start=(g == 0),
                         stop=(g == PASSES - 1),
                     )
-                nc.vector.tensor_tensor(
-                    out=res[:, n, :],
-                    in0=acc[:],
-                    in1=bias_all[:, c * HEAD_DIM : (c + 1) * HEAD_DIM],
-                    op=ALU.add,
-                )
+                bias = bias_all[:, c * HEAD_DIM : (c + 1) * HEAD_DIM]
+                nc.vector.tensor_tensor(out=res[:, n, :], in0=acc[:], in1=bias, op=ALU.add)
             head = outs[c // HEADS][b, c % HEADS].rearrange("(p i) d -> p i d", i=SEQ_TILES)
             nc.sync.dma_start(out=head[:, first : first + STORE_TILES, :], in_=res[:])
 

@@ -59,29 +59,32 @@ def tile_transformerblock_pa_kernel(
         w_sb = keep.tile([P, CHUNKS, ROW_TILES, D], BF16)
         bias_all = keep.tile([P, 3 * D], BF16)
 
-        def load_weights(c):
+        def load_tokens(j, n):
+            b, i = divmod(j, SEQ_TILES)
+            nc.sync.dma_start(out=x_sb[:, j : j + n, :], in_=x_view[:, b, i : i + n, :])
+
+        def load_weights(c, first, n):
             rows = in_proj_w[c * HEAD_DIM : (c + 1) * HEAD_DIM, :]
             nc.sync.dma_start(
-                out=w_sb[:, c, :, :], in_=rows.rearrange("(a p) k -> p a k", p=P)
+                out=w_sb[:, c, first : first + n, :],
+                in_=rows.rearrange("(p a) k -> p a k", a=ROW_TILES)[:, first : first + n, :],
             )
 
-        nc.sync.dma_start(out=x_sb[:, 0, :], in_=x_view[:, 0, 0, :])
+        load_tokens(0, 1)
         nc.sync.dma_start(out=gain_row[0:1, :], in_=w_norm1.unsqueeze(0))
-        for i in range(1, SEQ_TILES):
-            nc.sync.dma_start(out=x_sb[:, i, :], in_=x_view[:, 0, i, :])
-        load_weights(0)
-        load_weights(1)
+        load_tokens(1, 1)
+        load_weights(0, 0, 2)
+        load_tokens(2, 1)
+        load_weights(0, 2, 2)
+        load_tokens(3, 1)
+        load_weights(1, 0, ROW_TILES)
         nc.sync.dma_start(out=bias_all[:], in_=in_proj_b.partition_broadcast(P))
-        load_weights(2)
-        nc.sync.dma_start(
-            out=x_sb[:, SEQ_TILES + 0 : SEQ_TILES + 2, :], in_=x_view[:, 1, 0 : 2, :]
-        )
-        load_weights(3)
-        nc.sync.dma_start(
-            out=x_sb[:, SEQ_TILES + 2 : SEQ_TILES + 4, :], in_=x_view[:, 1, 2 : 4, :]
-        )
-        load_weights(4)
-        load_weights(5)
+        load_weights(2, 0, ROW_TILES)
+        load_tokens(SEQ_TILES, 2)
+        load_weights(3, 0, ROW_TILES)
+        load_tokens(SEQ_TILES + 2, 2)
+        load_weights(4, 0, ROW_TILES)
+        load_weights(5, 0, ROW_TILES)
 
         gain_all = const.tile([P, D], BF16)
         spread = turned.tile([P, D], BF16, tag="turned")
@@ -103,7 +106,7 @@ def tile_transformerblock_pa_kernel(
         h_grouped = {}
         w_grouped = {}
 
-        def normalise(j):
+        def measure(j):
             nc.scalar.activation(
                 out=squares[:, j, :],
                 in_=x_sb[:, j, :],
@@ -117,6 +120,8 @@ def tile_transformerblock_pa_kernel(
                 func=ACT.Abs_reciprocal_sqrt,
                 bias=eps[:, 0:1],
             )
+
+        def normalise(j):
             nc.vector.scalar_tensor_tensor(
                 out=h_sb[:, j, :],
                 in0=x_sb[:, j, :],
@@ -126,7 +131,7 @@ def tile_transformerblock_pa_kernel(
                 op1=ALU.mult,
             )
 
-        def turn_tokens(j):
+        def turn_tokens(j, empty=nc.scalar.copy):
             words = h_sb[:, j, :].bitcast(F32)
             bank = turned.tile([P, 2 * PASSES, P], F32, tag="turned")
             for s in range(2 * PASSES):
@@ -135,7 +140,7 @@ def tile_transformerblock_pa_kernel(
                     bank[:, s, :], words[:, 2 * g * P + u : 2 * (g + 1) * P : 2], ident[:]
                 )
             grouped = stage.tile([P, PASSES, P, 4], BF16, align_bytes=64, tag="h_grouped")
-            nc.scalar.copy(
+            empty(
                 out=grouped[:].bitcast(F32),
                 in_=bank[:].rearrange("p (g u) r -> p g r u", u=2),
             )
@@ -148,12 +153,16 @@ def tile_transformerblock_pa_kernel(
                 in_=h_grouped[j][:].rearrange("p g r t -> p (g r t)"),
             )
 
-        def turn_weights(c):
+        def turn_weights(c, banks=(0, 1, 2, 3), on_vector=()):
             words = w_sb[:, c, :, :].bitcast(F32)
-            grouped = stage.tile([P, PASSES, HEAD_DIM, 4], BF16, align_bytes=64, tag="w_grouped")
-            grouped_words = grouped[:].bitcast(F32)
-            for g in range(PASSES):
-                for pair in range(ROW_TILES // 2):
+            if c not in w_grouped:
+                w_grouped[c] = stage.tile(
+                    [P, PASSES, HEAD_DIM, 4], BF16, align_bytes=64, tag="w_grouped", name="w_grouped"
+                )
+            grouped_words = w_grouped[c][:].bitcast(F32)
+            for k in banks:
+                g, pair = divmod(k, 2)
+                if True:
                     bank = turned.tile([P, 4, P], F32, tag="turned")
                     for a in range(2):
                         for u in range(2):
@@ -162,13 +171,12 @@ def tile_transformerblock_pa_kernel(
                                 words[:, 2 * pair + a, 2 * g * P + u : 2 * (g + 1) * P : 2],
                                 ident[:],
                             )
-                    nc.scalar.copy(
+                    (nc.vector.tensor_copy if k in on_vector else nc.scalar.copy)(
                         out=grouped_words[:, g, pair * 2 * P : (pair + 1) * 2 * P, :].rearrange(
                             "p (a r) u -> p a r u", a=2
                         ),
                         in_=bank[:].rearrange("p (a u) r -> p a r u", u=2),
                     )
-            w_grouped[c] = grouped
 
         def quantise_weights(c):
             nc.vector.quantize_mx(
@@ -177,7 +185,7 @@ def tile_transformerblock_pa_kernel(
                 in_=w_grouped[c][:].rearrange("p g n t -> p (g n t)"),
             )
 
-        def project(c, b, part):
+        def project(c, b, part, stores=1):
             res = results.tile([P, STORE_TILES, HEAD_DIM], F32, tag="res")
             first = part * STORE_TILES
             for n in range(STORE_TILES):
@@ -194,17 +202,33 @@ def tile_transformerblock_pa_kernel(
                         stop=(g == PASSES - 1),
                     )
                 bias = bias_all[:, c * HEAD_DIM : (c + 1) * HEAD_DIM]
-                nc.vector.tensor_tensor(out=res[:, n, :], in0=acc[:], in1=bias, op=ALU.add)
+                nc.vector.tensor_tensor(
+                    out=res[:, n, :].rearrange("p (r a) -> p r a", a=ROW_TILES),
+                    in0=acc[:].rearrange("p (a r) -> p r a", a=ROW_TILES),
+                    in1=bias.rearrange("p (r a) -> p r a", a=ROW_TILES),
+                    op=ALU.add,
+                )
             head = outs[c // HEADS][b, c % HEADS].rearrange("(p i) d -> p i d", i=SEQ_TILES)
-            nc.sync.dma_start(out=head[:, first : first + STORE_TILES, :], in_=res[:])
+            width = STORE_TILES // stores
+            for n in range(0, STORE_TILES, width):
+                nc.sync.dma_start(
+                    out=head[:, first + n : first + n + width, :], in_=res[:, n : n + width, :]
+                )
 
+        measure(0)
         normalise(0)
+        measure(1)
         normalise(1)
+        turn_weights(0, (0,), (0, 1, 2, 3))
+        measure(2)
         normalise(2)
         turn_tokens(0)
+        turn_weights(0, (2,), (0, 1, 2, 3))
+        measure(3)
         normalise(3)
         turn_tokens(1)
-        turn_weights(0)
+        turn_weights(0, (1,))
+        turn_weights(0, (3,))
         quantise_tokens(0)
         quantise_tokens(1)
         turn_tokens(2)
@@ -217,17 +241,20 @@ def tile_transformerblock_pa_kernel(
             late = SEQ_TILES + c - 2
             if c + 1 < CHUNKS:
                 turn_weights(c + 1)
-            if c >= 2:
+            if SEQ_TILES <= late < TOKEN_TILES:
                 turn_tokens(late)
             project(c, 0, 0)
             if c + 1 < CHUNKS:
                 quantise_weights(c + 1)
             project(c, 0, 1)
-            if c >= 2:
+            if SEQ_TILES <= late < TOKEN_TILES:
                 quantise_tokens(late)
+            if c < SEQ_TILES:
+                measure(SEQ_TILES + c)
             if c < SEQ_TILES:
                 normalise(SEQ_TILES + c)
 
         for c in range(CHUNKS):
             for part in range(SEQ_TILES // STORE_TILES):
-                project(c, 1, part)
+                last = c == CHUNKS - 1 and part == 1
+                project(c, 1, part, stores=STORE_TILES if last else 1)

from contextlib import ExitStack

import concourse.mybir as mybir
from concourse.masks import make_identity

BF16 = mybir.dt.bfloat16
F32 = mybir.dt.float32
U32 = mybir.dt.uint32
U8 = mybir.dt.uint8
FP8X4 = mybir.dt.float8_e4m3fn_x4
ACT = mybir.ActivationFunctionType
ALU = mybir.AluOpType

P = 128
SEQ, BATCH, D, HEADS = 512, 2, 1024, 2
HEAD_DIM = D // HEADS
EPS = 1e-8

K_PASS = 4 * P
PASSES = D // K_PASS
WORDS = D // 2
SEQ_TILES = SEQ // P
TOKEN_TILES = BATCH * SEQ_TILES
CHUNKS = 3 * HEADS
ROW_TILES = HEAD_DIM // P
STORE_TILES = 2

FLOPS = 2 * SEQ * BATCH * D * 3 * D


def tile_transformerblock_pa_kernel(
    tc, x, w_norm1, in_proj_w, in_proj_b, out_0, out_1, out_2
):
    nc = tc.nc
    outs = (out_0, out_1, out_2)
    x_view = x.rearrange("(p i) b d -> p b i d", i=SEQ_TILES)

    with ExitStack() as ctx:
        const = ctx.enter_context(tc.tile_pool(name="const", bufs=1))
        keep = ctx.enter_context(tc.tile_pool(name="keep", bufs=1))
        stage = ctx.enter_context(tc.tile_pool(name="stage", bufs=2))
        results = ctx.enter_context(tc.tile_pool(name="results", bufs=6))
        turned = ctx.enter_context(tc.psum_pool(name="turned", bufs=4))
        sums = ctx.enter_context(tc.psum_pool(name="sums", bufs=4))
        ctx.enter_context(tc.manual_schedule())

        eps = const.tile([P, 1], F32)
        nc.vector.memset(eps[:], EPS)
        table_warm = const.tile([P, 1], F32)
        nc.scalar.activation(out=table_warm[:], in_=eps[:], func=ACT.Abs_reciprocal_sqrt)
        gain_row = const.tile([P, D], BF16)
        nc.vector.memset(gain_row[:].bitcast(F32), 0.0)
        ones = const.tile([P, P], BF16)
        nc.vector.memset(ones[:], 1.0)
        ident = const.tile([P, P], F32)
        make_identity(nc, ident[:])

        x_sb = keep.tile([P, TOKEN_TILES, D], BF16)
        w_sb = keep.tile([P, CHUNKS, ROW_TILES, D], BF16)
        bias_all = keep.tile([P, 3 * D], BF16)

        def load_tokens(j, n):
            b, i = divmod(j, SEQ_TILES)
            nc.sync.dma_start(out=x_sb[:, j : j + n, :], in_=x_view[:, b, i : i + n, :])

        def load_weights(c, first, n):
            rows = in_proj_w[c * HEAD_DIM : (c + 1) * HEAD_DIM, :]
            nc.sync.dma_start(
                out=w_sb[:, c, first : first + n, :],
                in_=rows.rearrange("(p a) k -> p a k", a=ROW_TILES)[:, first : first + n, :],
            )

        load_tokens(0, 1)
        nc.sync.dma_start(out=gain_row[0:1, :], in_=w_norm1.unsqueeze(0))
        load_tokens(1, 1)
        load_weights(0, 0, 2)
        load_tokens(2, 1)
        load_weights(0, 2, 2)
        load_tokens(3, 1)
        load_weights(1, 0, ROW_TILES)
        nc.sync.dma_start(out=bias_all[:], in_=in_proj_b.partition_broadcast(P))
        load_weights(2, 0, ROW_TILES)
        load_tokens(SEQ_TILES, 2)
        load_weights(3, 0, ROW_TILES)
        load_tokens(SEQ_TILES + 2, 2)
        load_weights(4, 0, ROW_TILES)
        load_weights(5, 0, ROW_TILES)

        gain_all = const.tile([P, D], BF16)
        spread = turned.tile([P, D], BF16, tag="turned")
        for half in range(D // HEAD_DIM):
            cols = slice(half * HEAD_DIM, (half + 1) * HEAD_DIM)
            nc.tensor.matmul(
                spread[:, cols], lhsT=ones[:], rhs=gain_row[:, cols], start=True, stop=True
            )
        nc.vector.tensor_copy(out=gain_all[:], in_=spread[:])

        squares = keep.tile([P, TOKEN_TILES, D], BF16)
        mean_sq = keep.tile([P, TOKEN_TILES], F32)
        inv_rms = keep.tile([P, TOKEN_TILES], F32)
        h_sb = keep.tile([P, TOKEN_TILES, D], BF16)
        h_codes = keep.tile([P, TOKEN_TILES, PASSES * P], U32, align_bytes=64)
        h_scales = keep.tile([P, TOKEN_TILES, PASSES * P], U8, align_bytes=64)
        w_codes = keep.tile([P, CHUNKS, PASSES * HEAD_DIM], U32, align_bytes=64)
        w_scales = keep.tile([P, CHUNKS, PASSES * HEAD_DIM], U8, align_bytes=64)
        h_grouped = {}
        w_grouped = {}

        def measure(j):
            nc.scalar.activation(
                out=squares[:, j, :],
                in_=x_sb[:, j, :],
                func=ACT.Square,
                scale=D**-0.5,
                accum_out=mean_sq[:, j : j + 1],
            )
            nc.scalar.activation(
                out=inv_rms[:, j : j + 1],
                in_=mean_sq[:, j : j + 1],
                func=ACT.Abs_reciprocal_sqrt,
                bias=eps[:, 0:1],
            )

        def normalise(j):
            nc.vector.scalar_tensor_tensor(
                out=h_sb[:, j, :],
                in0=x_sb[:, j, :],
                scalar=inv_rms[:, j : j + 1],
                in1=gain_all[:],
                op0=ALU.mult,
                op1=ALU.mult,
            )

        def turn_tokens(j, empty=nc.scalar.copy):
            words = h_sb[:, j, :].bitcast(F32)
            bank = turned.tile([P, 2 * PASSES, P], F32, tag="turned")
            for s in range(2 * PASSES):
                g, u = divmod(s, 2)
                nc.tensor.transpose(
                    bank[:, s, :], words[:, 2 * g * P + u : 2 * (g + 1) * P : 2], ident[:]
                )
            grouped = stage.tile([P, PASSES, P, 4], BF16, align_bytes=64, tag="h_grouped")
            empty(
                out=grouped[:].bitcast(F32),
                in_=bank[:].rearrange("p (g u) r -> p g r u", u=2),
            )
            h_grouped[j] = grouped

        def quantise_tokens(j):
            nc.vector.quantize_mx(
                out=h_codes[:, j, :].bitcast(FP8X4),
                scales=h_scales[:, j, :],
                in_=h_grouped[j][:].rearrange("p g r t -> p (g r t)"),
            )

        def turn_weights(c, banks=(0, 1, 2, 3), on_vector=()):
            words = w_sb[:, c, :, :].bitcast(F32)
            if c not in w_grouped:
                w_grouped[c] = stage.tile(
                    [P, PASSES, HEAD_DIM, 4], BF16, align_bytes=64, tag="w_grouped", name="w_grouped"
                )
            grouped_words = w_grouped[c][:].bitcast(F32)
            for k in banks:
                g, pair = divmod(k, 2)
                if True:
                    bank = turned.tile([P, 4, P], F32, tag="turned")
                    for a in range(2):
                        for u in range(2):
                            nc.tensor.transpose(
                                bank[:, 2 * a + u, :],
                                words[:, 2 * pair + a, 2 * g * P + u : 2 * (g + 1) * P : 2],
                                ident[:],
                            )
                    (nc.vector.tensor_copy if k in on_vector else nc.scalar.copy)(
                        out=grouped_words[:, g, pair * 2 * P : (pair + 1) * 2 * P, :].rearrange(
                            "p (a r) u -> p a r u", a=2
                        ),
                        in_=bank[:].rearrange("p (a u) r -> p a r u", u=2),
                    )

        def quantise_weights(c):
            nc.vector.quantize_mx(
                out=w_codes[:, c, :].bitcast(FP8X4),
                scales=w_scales[:, c, :],
                in_=w_grouped[c][:].rearrange("p g n t -> p (g n t)"),
            )

        def project(c, b, part, stores=1):
            res = results.tile([P, STORE_TILES, HEAD_DIM], F32, tag="res")
            first = part * STORE_TILES
            for n in range(STORE_TILES):
                j = b * SEQ_TILES + first + n
                acc = sums.tile([P, HEAD_DIM], F32, tag="acc")
                for g in range(PASSES):
                    nc.tensor.matmul_mx(
                        out=acc[:],
                        lhsT=h_codes[:, j, g * P : (g + 1) * P].bitcast(FP8X4),
                        lhsT_scale=h_scales[:, j, g * P : (g + 1) * P],
                        rhs=w_codes[:, c, g * HEAD_DIM : (g + 1) * HEAD_DIM].bitcast(FP8X4),
                        rhs_scale=w_scales[:, c, g * HEAD_DIM : (g + 1) * HEAD_DIM],
                        start=(g == 0),
                        stop=(g == PASSES - 1),
                    )
                bias = bias_all[:, c * HEAD_DIM : (c + 1) * HEAD_DIM]
                nc.vector.tensor_tensor(
                    out=res[:, n, :].rearrange("p (r a) -> p r a", a=ROW_TILES),
                    in0=acc[:].rearrange("p (a r) -> p r a", a=ROW_TILES),
                    in1=bias.rearrange("p (r a) -> p r a", a=ROW_TILES),
                    op=ALU.add,
                )
            head = outs[c // HEADS][b, c % HEADS].rearrange("(p i) d -> p i d", i=SEQ_TILES)
            width = STORE_TILES // stores
            for n in range(0, STORE_TILES, width):
                nc.sync.dma_start(
                    out=head[:, first + n : first + n + width, :], in_=res[:, n : n + width, :]
                )

        measure(0)
        normalise(0)
        measure(1)
        normalise(1)
        turn_weights(0, (0,), (0, 1, 2, 3))
        measure(2)
        normalise(2)
        turn_tokens(0)
        turn_weights(0, (2,), (0, 1, 2, 3))
        measure(3)
        normalise(3)
        turn_tokens(1)
        turn_weights(0, (1,))
        turn_weights(0, (3,))
        quantise_tokens(0)
        quantise_tokens(1)
        turn_tokens(2)
        turn_tokens(3)
        quantise_weights(0)
        quantise_tokens(2)
        quantise_tokens(3)

        for c in range(CHUNKS):
            late = SEQ_TILES + c - 2
            if c + 1 < CHUNKS:
                turn_weights(c + 1)
            if SEQ_TILES <= late < TOKEN_TILES:
                turn_tokens(late)
            project(c, 0, 0)
            if c + 1 < CHUNKS:
                quantise_weights(c + 1)
            project(c, 0, 1)
            if SEQ_TILES <= late < TOKEN_TILES:
                quantise_tokens(late)
            if c < SEQ_TILES:
                measure(SEQ_TILES + c)
            if c < SEQ_TILES:
                normalise(SEQ_TILES + c)

        for c in range(CHUNKS):
            for part in range(SEQ_TILES // STORE_TILES):
                last = c == CHUNKS - 1 and part == 1
                project(c, 1, part, stores=STORE_TILES if last else 1)
